import numpy as np
import ml_dtypes


def mxq(x, axis, fmt="e4m3"):
    dtype, down = {"e4m3": (ml_dtypes.float8_e4m3fn, 7), "e5m2": (ml_dtypes.float8_e5m2, 14)}[fmt]
    v = np.moveaxis(np.asarray(x, np.float32).astype(ml_dtypes.bfloat16).astype(np.float64), axis, -1)
    blocks = v.reshape(v.shape[:-1] + (-1, 32))
    amax = np.abs(blocks).max(-1, keepdims=True)
    byte = np.maximum(np.where(amax > 0, np.frexp(amax)[1] - 1 + 127, 0) - down, 1)
    scale = np.exp2(byte - 127.0)
    codes = (blocks / scale).astype(np.float32).astype(dtype).astype(np.float64)
    return np.moveaxis((codes * scale).reshape(v.shape), -1, axis)


WIDE = False


def mx_kscale(k):
    if not WIDE:
        return np.ones(k)
    levels = np.array([10, -10, 5, -5, 0])
    a = np.random.permutation(np.resize(levels, k // 512 * 4)).reshape(k // 512, 4)
    idx = np.arange(k)
    return np.exp2(a[idx // 512, idx % 128 // 32])


BF16 = ml_dtypes.bfloat16


def bf(x):
    return np.asarray(x, np.float32).astype(BF16)


def f64(x):
    return np.asarray(x).astype(np.float64)


B, C, O, E = 32, 512, 128, 2
KERNEL = 3
PADDING = 1


def setup_inputs():
    s = mx_kscale(C)
    return {"x": bf(np.random.standard_normal((B, C, E, E)) * s[None, :, None, None]),
            "weights": bf(np.random.random((E, E, O, C, KERNEL, KERNEL)) * 1.7 / np.sqrt(KERNEL * KERNEL * C) / s[None, None, None, :, None, None])}


def reference(x, weights):
    xq = mxq(f64(x), 1, "e4m3")
    wt = f64(weights)
    out = np.zeros((B, O, E, E))
    for i in range(KERNEL):
        for j in range(KERNEL):
            w0, w1 = max(0, PADDING - i), min(E, E + PADDING - i)
            h0, h1 = max(0, PADDING - j), min(E, E + PADDING - j)
            wq = mxq(wt[h0:h1, w0:w1, :, :, i, j], 3, "e4m3").transpose(0, 1, 3, 2)
            xs = xq[:, :, w0 + i - PADDING:w1 + i - PADDING, h0 + j - PADDING:h1 + j - PADDING].transpose(3, 2, 0, 1)
            out[:, :, h0:h1, w0:w1] += (xs @ wq).transpose(2, 3, 0, 1)
    return out

@@ -1,0 +1,132 @@
+from contextlib import ExitStack
+
+import concourse.mybir as mybir
+from concourse.masks import make_identity
+
+F32 = mybir.dt.float32
+BF16 = mybir.dt.bfloat16
+I32 = mybir.dt.int32
+U32 = mybir.dt.uint32
+U8 = mybir.dt.uint8
+FP8X4 = mybir.dt.float8_e4m3fn_x4
+
+B, C, O, E, KERNEL = 32, 512, 128, 2, 3
+P = 128
+PACK = 4
+TAPS = E * E
+PLACES = E * E
+C_PASS = P * PACK // TAPS
+PASSES = C // C_PASS
+HALF = 2
+ROUNDS = PASSES // HALF
+RAW_COLS = HALF * C_PASS * KERNEL * KERNEL
+
+FLOPS = 2 * B * O * PLACES * TAPS * C
+BYTES = 2 * (PLACES * TAPS * O * C) + 2 * (B * C * TAPS) + 4 * (B * O * PLACES)
+
+
+def tile_locallyconnected2d_s_kernel(tc, x, weights, out):
+    nc = tc.nc
+    with ExitStack() as ctx:
+        keep = ctx.enter_context(tc.tile_pool(name="keep", bufs=1))
+        raw_pool = ctx.enter_context(tc.tile_pool(name="raw", bufs=PLACES * ROUNDS))
+        work = ctx.enter_context(tc.tile_pool(name="work", bufs=3))
+        psum_t = ctx.enter_context(tc.psum_pool(name="psum_t", bufs=4))
+        psum_keep = ctx.enter_context(tc.psum_pool(name="psum_keep", bufs=1))
+
+        x_raw = keep.tile([P, C_PASS * TAPS], BF16)
+        nc.sync.dma_start(
+            out=x_raw[:], in_=x.rearrange("b (g c) r q -> (b g) (c r q)", g=PASSES)
+        )
+        w_raw = {}
+        for h in range(E):
+            for w in range(E):
+                rows = weights[h, w].rearrange("o c i j -> o (c i j)")
+                for n in range(ROUNDS):
+                    w_raw[h, w, n] = raw_pool.tile([P, RAW_COLS], BF16, name="w_raw")
+                    nc.sync.dma_start(
+                        out=w_raw[h, w, n][:], in_=rows[:, n * RAW_COLS : (n + 1) * RAW_COLS]
+                    )
+
+        ident = keep.tile([P, P], F32)
+        make_identity(nc, ident[:])
+
+        x_grouped = keep.tile([P, PASSES * P * PACK], BF16, align_bytes=64)
+        nc.vector.memset(x_grouped[:].bitcast(I32), 0)
+
+        x_sorted = keep.tile([P, TAPS * C_PASS], BF16)
+        nc.vector.tensor_copy(
+            out=x_sorted[:].rearrange("p (t c) -> p t c", t=TAPS),
+            in_=x_raw[:].rearrange("p (c t) -> p t c", t=TAPS),
+        )
+        x_words = x_sorted[:].bitcast(F32).rearrange("p (m u) -> p u m", u=2)
+        x_ps = psum_keep.tile([P, 2, P], F32)
+        for u in range(2):
+            nc.tensor.transpose(x_ps[:, u, :], x_words[:, u, :], ident[:])
+        nc.scalar.copy(
+            out=x_grouped[:]
+            .bitcast(F32)
+            .rearrange("p (g b u) -> p g b u", g=PASSES, u=2)[:, :, 0:B, :],
+            in_=x_ps[:].rearrange("p u (b g) -> p g b u", g=PASSES),
+        )
+        x_codes = keep.tile([P, PASSES, P], U32, align_bytes=64)
+        x_scales = keep.tile([P, PASSES, P], U8, align_bytes=64)
+        nc.vector.quantize_mx(
+            out=x_codes[:].rearrange("p g b -> p (g b)").bitcast(FP8X4),
+            scales=x_scales[:].rearrange("p g b -> p (g b)"),
+            in_=x_grouped[:],
+        )
+
+        acc = psum_keep.tile([P, PLACES, O], F32)
+        for h in range(E):
+            for w in range(E):
+                i0, j0 = 1 - w, 1 - h
+                for n in range(ROUNDS):
+                    w_sorted = work.tile([P, HALF * TAPS * C_PASS], BF16)
+                    nc.vector.tensor_copy(
+                        out=w_sorted[:].rearrange(
+                            "o (g i j c) -> o g i c j", g=HALF, i=E, j=E
+                        ),
+                        in_=w_raw[h, w, n][:].rearrange(
+                            "o (g c i j) -> o g i c j", g=HALF, i=KERNEL, j=KERNEL
+                        )[:, :, i0 : i0 + E, :, j0 : j0 + E],
+                    )
+                    w_words = w_sorted[:].bitcast(F32).rearrange(
+                        "o (g m u) -> o g u m", g=HALF, u=2
+                    )
+                    w_ps = psum_t.tile([P, HALF, 2, O], F32)
+                    for g in range(HALF):
+                        for u in range(2):
+                            nc.tensor.transpose(w_ps[:, g, u, :], w_words[:, g, u, :], ident[:])
+                    w_grouped = work.tile([P, HALF * O * PACK], BF16, align_bytes=64)
+                    nc.scalar.copy(
+                        out=w_grouped[:]
+                        .bitcast(F32)
+                        .rearrange("p (g o u) -> p g o u", g=HALF, u=2),
+                        in_=w_ps[:].rearrange("p g u o -> p g o u"),
+                    )
+                    w_codes = work.tile([P, HALF, O], U32, align_bytes=64)
+                    w_scales = work.tile([P, HALF, O], U8, align_bytes=64)
+                    nc.vector.quantize_mx(
+                        out=w_codes[:].rearrange("p g o -> p (g o)").bitcast(FP8X4),
+                        scales=w_scales[:].rearrange("p g o -> p (g o)"),
+                        in_=w_grouped[:],
+                    )
+                    for g in range(HALF):
+                        k = n * HALF + g
+                        nc.tensor.matmul_mx(
+                            out=acc[:, h * E + w, :],
+                            lhsT=x_codes[:, k, :].bitcast(FP8X4),
+                            lhsT_scale=x_scales[:, k, :],
+                            rhs=w_codes[:, g, :].bitcast(FP8X4),
+                            rhs_scale=w_scales[:, g, :],
+                            start=(k == 0),
+                            stop=(k == PASSES - 1),
+                        )
+
+        result = keep.tile([B, O, PLACES], F32)
+        nc.scalar.copy(out=result[:], in_=acc[0:B, :, :].rearrange("b s o -> b o s"))
+        nc.sync.dma_start(
+            out=out.rearrange("b o h w -> b (o h w)"),
+            in_=result[:].rearrange("b o s -> b (o s)"),
+        )

@@ -29,9 +29,8 @@ def tile_locallyconnected2d_s_kernel(tc, x, weights, out):
     nc = tc.nc
     with ExitStack() as ctx:
         keep = ctx.enter_context(tc.tile_pool(name="keep", bufs=1))
-        raw_pool = ctx.enter_context(tc.tile_pool(name="raw", bufs=PLACES * ROUNDS))
-        work = ctx.enter_context(tc.tile_pool(name="work", bufs=3))
-        psum_t = ctx.enter_context(tc.psum_pool(name="psum_t", bufs=4))
+        per_round = ctx.enter_context(tc.tile_pool(name="per_round", bufs=PLACES * ROUNDS))
+        psum_t = ctx.enter_context(tc.psum_pool(name="psum_t", bufs=5))
         psum_keep = ctx.enter_context(tc.psum_pool(name="psum_keep", bufs=1))
 
         x_raw = keep.tile([P, C_PASS * TAPS], BF16)
@@ -43,13 +42,15 @@ def tile_locallyconnected2d_s_kernel(tc, x, weights, out):
             for w in range(E):
                 rows = weights[h, w].rearrange("o c i j -> o (c i j)")
                 for n in range(ROUNDS):
-                    w_raw[h, w, n] = raw_pool.tile([P, RAW_COLS], BF16, name="w_raw")
+                    w_raw[h, w, n] = per_round.tile([P, RAW_COLS], BF16, name="w_raw")
                     nc.sync.dma_start(
                         out=w_raw[h, w, n][:], in_=rows[:, n * RAW_COLS : (n + 1) * RAW_COLS]
                     )
 
         ident = keep.tile([P, P], F32)
         make_identity(nc, ident[:])
+
+        ctx.enter_context(tc.manual_schedule())
 
         x_grouped = keep.tile([P, PASSES * P * PACK], BF16, align_bytes=64)
         nc.vector.memset(x_grouped[:].bitcast(I32), 0)
@@ -71,58 +72,74 @@ def tile_locallyconnected2d_s_kernel(tc, x, weights, out):
         )
         x_codes = keep.tile([P, PASSES, P], U32, align_bytes=64)
         x_scales = keep.tile([P, PASSES, P], U8, align_bytes=64)
-        nc.vector.quantize_mx(
-            out=x_codes[:].rearrange("p g b -> p (g b)").bitcast(FP8X4),
-            scales=x_scales[:].rearrange("p g b -> p (g b)"),
-            in_=x_grouped[:],
-        )
+
+        def quantise_x():
+            nc.vector.quantize_mx(
+                out=x_codes[:].rearrange("p g b -> p (g b)").bitcast(FP8X4),
+                scales=x_scales[:].rearrange("p g b -> p (g b)"),
+                in_=x_grouped[:],
+            )
 
         acc = psum_keep.tile([P, PLACES, O], F32)
-        for h in range(E):
-            for w in range(E):
-                i0, j0 = 1 - w, 1 - h
-                for n in range(ROUNDS):
-                    w_sorted = work.tile([P, HALF * TAPS * C_PASS], BF16)
-                    nc.vector.tensor_copy(
-                        out=w_sorted[:].rearrange(
-                            "o (g i j c) -> o g i c j", g=HALF, i=E, j=E
-                        ),
-                        in_=w_raw[h, w, n][:].rearrange(
-                            "o (g c i j) -> o g i c j", g=HALF, i=KERNEL, j=KERNEL
-                        )[:, :, i0 : i0 + E, :, j0 : j0 + E],
-                    )
-                    w_words = w_sorted[:].bitcast(F32).rearrange(
-                        "o (g m u) -> o g u m", g=HALF, u=2
-                    )
-                    w_ps = psum_t.tile([P, HALF, 2, O], F32)
-                    for g in range(HALF):
-                        for u in range(2):
-                            nc.tensor.transpose(w_ps[:, g, u, :], w_words[:, g, u, :], ident[:])
-                    w_grouped = work.tile([P, HALF * O * PACK], BF16, align_bytes=64)
-                    nc.scalar.copy(
-                        out=w_grouped[:]
-                        .bitcast(F32)
-                        .rearrange("p (g o u) -> p g o u", g=HALF, u=2),
-                        in_=w_ps[:].rearrange("p g u o -> p g o u"),
-                    )
-                    w_codes = work.tile([P, HALF, O], U32, align_bytes=64)
-                    w_scales = work.tile([P, HALF, O], U8, align_bytes=64)
-                    nc.vector.quantize_mx(
-                        out=w_codes[:].rearrange("p g o -> p (g o)").bitcast(FP8X4),
-                        scales=w_scales[:].rearrange("p g o -> p (g o)"),
-                        in_=w_grouped[:],
-                    )
-                    for g in range(HALF):
-                        k = n * HALF + g
-                        nc.tensor.matmul_mx(
-                            out=acc[:, h * E + w, :],
-                            lhsT=x_codes[:, k, :].bitcast(FP8X4),
-                            lhsT_scale=x_scales[:, k, :],
-                            rhs=w_codes[:, g, :].bitcast(FP8X4),
-                            rhs_scale=w_scales[:, g, :],
-                            start=(k == 0),
-                            stop=(k == PASSES - 1),
-                        )
+        w_grouped = {}
+
+        def transpose_place(h, w):
+            i0, j0 = 1 - w, 1 - h
+            for n in range(ROUNDS):
+                w_sorted = per_round.tile([P, HALF * TAPS * C_PASS], BF16)
+                nc.vector.tensor_copy(
+                    out=w_sorted[:].rearrange("o (g i j c) -> o g i c j", g=HALF, i=E, j=E),
+                    in_=w_raw[h, w, n][:].rearrange(
+                        "o (g c i j) -> o g i c j", g=HALF, i=KERNEL, j=KERNEL
+                    )[:, :, i0 : i0 + E, :, j0 : j0 + E],
+                )
+                w_words = w_sorted[:].bitcast(F32).rearrange(
+                    "o (g m u) -> o g u m", g=HALF, u=2
+                )
+                w_ps = psum_t.tile([P, HALF, 2, O], F32)
+                for g in range(HALF):
+                    for u in range(2):
+                        nc.tensor.transpose(w_ps[:, g, u, :], w_words[:, g, u, :], ident[:])
+                w_grouped[h, w, n] = per_round.tile(
+                    [P, HALF * O * PACK], BF16, align_bytes=64, name="w_grouped"
+                )
+                nc.scalar.copy(
+                    out=w_grouped[h, w, n][:]
+                    .bitcast(F32)
+                    .rearrange("p (g o u) -> p g o u", g=HALF, u=2),
+                    in_=w_ps[:].rearrange("p g u o -> p g o u"),
+                )
+
+        def multiply_place(h, w):
+            w_codes = {}
+            w_scales = {}
+            for n in range(ROUNDS):
+                w_codes[n] = per_round.tile([P, HALF, O], U32, align_bytes=64, name="w_codes")
+                w_scales[n] = per_round.tile([P, HALF, O], U8, align_bytes=64, name="w_scales")
+                nc.vector.quantize_mx(
+                    out=w_codes[n][:].rearrange("p g o -> p (g o)").bitcast(FP8X4),
+                    scales=w_scales[n][:].rearrange("p g o -> p (g o)"),
+                    in_=w_grouped[h, w, n][:],
+                )
+            for k in range(PASSES):
+                n, g = divmod(k, HALF)
+                nc.tensor.matmul_mx(
+                    out=acc[:, h * E + w, :],
+                    lhsT=x_codes[:, k, :].bitcast(FP8X4),
+                    lhsT_scale=x_scales[:, k, :],
+                    rhs=w_codes[n][:, g, :].bitcast(FP8X4),
+                    rhs_scale=w_scales[n][:, g, :],
+                    start=(k == 0),
+                    stop=(k == PASSES - 1),
+                )
+
+        places = [(h, w) for h in range(E) for w in range(E)]
+        transpose_place(*places[0])
+        quantise_x()
+        for s in range(1, PLACES):
+            transpose_place(*places[s])
+            multiply_place(*places[s - 1])
+        multiply_place(*places[PLACES - 1])
 
         result = keep.tile([B, O, PLACES], F32)
         nc.scalar.copy(out=result[:], in_=acc[0:B, :, :].rearrange("b s o -> b o s"))

@@ -15,11 +15,11 @@ P = 128
 PACK = 4
 TAPS = E * E
 PLACES = E * E
-C_PASS = P * PACK // TAPS
-PASSES = C // C_PASS
-HALF = 2
-ROUNDS = PASSES // HALF
-RAW_COLS = HALF * C_PASS * KERNEL * KERNEL
+C_ROUND = P * PACK // E
+ROUNDS = C // C_ROUND
+PASSES = ROUNDS * E
+C_ROW = C_ROUND // 2
+RAW_COLS = C_ROUND * KERNEL * KERNEL
 
 FLOPS = 2 * B * O * PLACES * TAPS * C
 BYTES = 2 * (PLACES * TAPS * O * C) + 2 * (B * C * TAPS) + 4 * (B * O * PLACES)
@@ -33,9 +33,9 @@ def tile_locallyconnected2d_s_kernel(tc, x, weights, out):
         psum_t = ctx.enter_context(tc.psum_pool(name="psum_t", bufs=5))
         psum_keep = ctx.enter_context(tc.psum_pool(name="psum_keep", bufs=1))
 
-        x_raw = keep.tile([P, C_PASS * TAPS], BF16)
+        x_raw = keep.tile([P, C_ROW * TAPS], BF16)
         nc.sync.dma_start(
-            out=x_raw[:], in_=x.rearrange("b (g c) r q -> (b g) (c r q)", g=PASSES)
+            out=x_raw[:], in_=x.rearrange("b (g c) r q -> (b g) (c r q)", c=C_ROW)
         )
         w_raw = {}
         for h in range(E):
@@ -55,21 +55,22 @@ def tile_locallyconnected2d_s_kernel(tc, x, weights, out):
         x_grouped = keep.tile([P, PASSES * P * PACK], BF16, align_bytes=64)
         nc.vector.memset(x_grouped[:].bitcast(I32), 0)
 
-        x_sorted = keep.tile([P, TAPS * C_PASS], BF16)
+        x_sorted = keep.tile([P, TAPS * C_ROW], BF16)
         nc.vector.tensor_copy(
             out=x_sorted[:].rearrange("p (t c) -> p t c", t=TAPS),
             in_=x_raw[:].rearrange("p (c t) -> p t c", t=TAPS),
         )
-        x_words = x_sorted[:].bitcast(F32).rearrange("p (m u) -> p u m", u=2)
-        x_ps = psum_keep.tile([P, 2, P], F32)
-        for u in range(2):
-            nc.tensor.transpose(x_ps[:, u, :], x_words[:, u, :], ident[:])
-        nc.scalar.copy(
-            out=x_grouped[:]
-            .bitcast(F32)
-            .rearrange("p (g b u) -> p g b u", g=PASSES, u=2)[:, :, 0:B, :],
-            in_=x_ps[:].rearrange("p u (b g) -> p g b u", g=PASSES),
-        )
+        x_words = x_sorted[:].bitcast(F32).rearrange("p (r m) -> p r m", r=E)
+        x_ps = psum_keep.tile([P, E, P], F32)
+        for r in range(E):
+            nc.tensor.transpose(x_ps[:, r, :], x_words[:, r, :], ident[:])
+        for r in range(E):
+            nc.scalar.copy(
+                out=x_grouped[:]
+                .bitcast(F32)
+                .rearrange("p (n r b u) -> p r n b u", n=ROUNDS, r=E, u=2)[:, r, :, 0:B, :],
+                in_=x_ps[:, r, :].rearrange("p (b n u) -> p n b u", n=ROUNDS, u=2),
+            )
         x_codes = keep.tile([P, PASSES, P], U32, align_bytes=64)
         x_scales = keep.tile([P, PASSES, P], U8, align_bytes=64)
 
@@ -86,49 +87,47 @@ def tile_locallyconnected2d_s_kernel(tc, x, weights, out):
         def transpose_place(h, w):
             i0, j0 = 1 - w, 1 - h
             for n in range(ROUNDS):
-                w_sorted = per_round.tile([P, HALF * TAPS * C_PASS], BF16)
+                w_sorted = per_round.tile([P, TAPS * C_ROUND], BF16)
                 nc.vector.tensor_copy(
-                    out=w_sorted[:].rearrange("o (g i j c) -> o g i c j", g=HALF, i=E, j=E),
+                    out=w_sorted[:].rearrange("o (g i j c) -> o g i c j", g=2, i=E, j=E),
                     in_=w_raw[h, w, n][:].rearrange(
-                        "o (g c i j) -> o g i c j", g=HALF, i=KERNEL, j=KERNEL
+                        "o (g c i j) -> o g i c j", g=2, i=KERNEL, j=KERNEL
                     )[:, :, i0 : i0 + E, :, j0 : j0 + E],
                 )
-                w_words = w_sorted[:].bitcast(F32).rearrange(
-                    "o (g m u) -> o g u m", g=HALF, u=2
-                )
-                w_ps = psum_t.tile([P, HALF, 2, O], F32)
-                for g in range(HALF):
-                    for u in range(2):
-                        nc.tensor.transpose(w_ps[:, g, u, :], w_words[:, g, u, :], ident[:])
+                w_words = w_sorted[:].bitcast(F32).rearrange("o (g r m) -> o g r m", g=2, r=E)
+                w_ps = psum_t.tile([P, E, 2, O], F32)
+                for r in range(E):
+                    for g in range(2):
+                        nc.tensor.transpose(w_ps[:, r, g, :], w_words[:, g, r, :], ident[:])
                 w_grouped[h, w, n] = per_round.tile(
-                    [P, HALF * O * PACK], BF16, align_bytes=64, name="w_grouped"
+                    [P, E * O * PACK], BF16, align_bytes=64, name="w_grouped"
                 )
                 nc.scalar.copy(
                     out=w_grouped[h, w, n][:]
                     .bitcast(F32)
-                    .rearrange("p (g o u) -> p g o u", g=HALF, u=2),
-                    in_=w_ps[:].rearrange("p g u o -> p g o u"),
+                    .rearrange("p (r o g) -> p r o g", r=E, g=2),
+                    in_=w_ps[:].rearrange("p r g o -> p r o g"),
                 )
 
         def multiply_place(h, w):
             w_codes = {}
             w_scales = {}
             for n in range(ROUNDS):
-                w_codes[n] = per_round.tile([P, HALF, O], U32, align_bytes=64, name="w_codes")
-                w_scales[n] = per_round.tile([P, HALF, O], U8, align_bytes=64, name="w_scales")
+                w_codes[n] = per_round.tile([P, E, O], U32, align_bytes=64, name="w_codes")
+                w_scales[n] = per_round.tile([P, E, O], U8, align_bytes=64, name="w_scales")
                 nc.vector.quantize_mx(
-                    out=w_codes[n][:].rearrange("p g o -> p (g o)").bitcast(FP8X4),
-                    scales=w_scales[n][:].rearrange("p g o -> p (g o)"),
+                    out=w_codes[n][:].rearrange("p r o -> p (r o)").bitcast(FP8X4),
+                    scales=w_scales[n][:].rearrange("p r o -> p (r o)"),
                     in_=w_grouped[h, w, n][:],
                 )
             for k in range(PASSES):
-                n, g = divmod(k, HALF)
+                n, r = divmod(k, E)
                 nc.tensor.matmul_mx(
                     out=acc[:, h * E + w, :],
                     lhsT=x_codes[:, k, :].bitcast(FP8X4),
                     lhsT_scale=x_scales[:, k, :],
-                    rhs=w_codes[n][:, g, :].bitcast(FP8X4),
-                    rhs_scale=w_scales[n][:, g, :],
+                    rhs=w_codes[n][:, r, :].bitcast(FP8X4),
+                    rhs_scale=w_scales[n][:, r, :],
                     start=(k == 0),
                     stop=(k == PASSES - 1),
                 )

@@ -15,11 +15,12 @@ P = 128
 PACK = 4
 TAPS = E * E
 PLACES = E * E
-C_ROUND = P * PACK // E
-ROUNDS = C // C_ROUND
-PASSES = ROUNDS * E
-C_ROW = C_ROUND // 2
-RAW_COLS = C_ROUND * KERNEL * KERNEL
+C_PASS = P * PACK // TAPS
+PASSES = C // C_PASS
+RAW_COLS = C_PASS * KERNEL * KERNEL
+PAIR = 2
+ROUNDS = PLACES * PASSES // PAIR
+LAG = 2
 
 FLOPS = 2 * B * O * PLACES * TAPS * C
 BYTES = 2 * (PLACES * TAPS * O * C) + 2 * (B * C * TAPS) + 4 * (B * O * PLACES)
@@ -29,23 +30,27 @@ def tile_locallyconnected2d_s_kernel(tc, x, weights, out):
     nc = tc.nc
     with ExitStack() as ctx:
         keep = ctx.enter_context(tc.tile_pool(name="keep", bufs=1))
-        per_round = ctx.enter_context(tc.tile_pool(name="per_round", bufs=PLACES * ROUNDS))
-        psum_t = ctx.enter_context(tc.psum_pool(name="psum_t", bufs=5))
+        per_pass = ctx.enter_context(tc.tile_pool(name="per_pass", bufs=PLACES * PASSES))
+        psum_t = ctx.enter_context(tc.psum_pool(name="psum_t", bufs=6))
         psum_keep = ctx.enter_context(tc.psum_pool(name="psum_keep", bufs=1))
 
-        x_raw = keep.tile([P, C_ROW * TAPS], BF16)
+        x_raw = keep.tile([P, C_PASS * TAPS], BF16)
         nc.sync.dma_start(
-            out=x_raw[:], in_=x.rearrange("b (g c) r q -> (b g) (c r q)", c=C_ROW)
+            out=x_raw[:], in_=x.rearrange("b (k c) r q -> (b k) (c r q)", k=PASSES)
         )
+        w_rows = weights.rearrange("h w o c i j -> (h w) o (c i j)")
         w_raw = {}
-        for h in range(E):
-            for w in range(E):
-                rows = weights[h, w].rearrange("o c i j -> o (c i j)")
-                for n in range(ROUNDS):
-                    w_raw[h, w, n] = per_round.tile([P, RAW_COLS], BF16, name="w_raw")
-                    nc.sync.dma_start(
-                        out=w_raw[h, w, n][:], in_=rows[:, n * RAW_COLS : (n + 1) * RAW_COLS]
-                    )
+        for n in range(ROUNDS):
+            passes_a_load = 1 if n == ROUNDS - 1 else PAIR
+            for first in range(PAIR * n, PAIR * (n + 1), passes_a_load):
+                s, k = divmod(first, PASSES)
+                w_load = per_pass.tile([P, passes_a_load * RAW_COLS], BF16)
+                nc.sync.dma_start(
+                    out=w_load[:],
+                    in_=w_rows[s, :, k * RAW_COLS : (k + passes_a_load) * RAW_COLS],
+                )
+                for g in range(passes_a_load):
+                    w_raw[first + g] = w_load[:, g * RAW_COLS : (g + 1) * RAW_COLS]
 
         ident = keep.tile([P, P], F32)
         make_identity(nc, ident[:])
@@ -55,90 +60,81 @@ def tile_locallyconnected2d_s_kernel(tc, x, weights, out):
         x_grouped = keep.tile([P, PASSES * P * PACK], BF16, align_bytes=64)
         nc.vector.memset(x_grouped[:].bitcast(I32), 0)
 
-        x_sorted = keep.tile([P, TAPS * C_ROW], BF16)
+        x_sorted = keep.tile([P, TAPS * C_PASS], BF16)
         nc.vector.tensor_copy(
             out=x_sorted[:].rearrange("p (t c) -> p t c", t=TAPS),
             in_=x_raw[:].rearrange("p (c t) -> p t c", t=TAPS),
         )
-        x_words = x_sorted[:].bitcast(F32).rearrange("p (r m) -> p r m", r=E)
-        x_ps = psum_keep.tile([P, E, P], F32)
-        for r in range(E):
-            nc.tensor.transpose(x_ps[:, r, :], x_words[:, r, :], ident[:])
-        for r in range(E):
-            nc.scalar.copy(
-                out=x_grouped[:]
-                .bitcast(F32)
-                .rearrange("p (n r b u) -> p r n b u", n=ROUNDS, r=E, u=2)[:, r, :, 0:B, :],
-                in_=x_ps[:, r, :].rearrange("p (b n u) -> p n b u", n=ROUNDS, u=2),
-            )
+        x_words = x_sorted[:].bitcast(F32).rearrange("p (m u) -> p u m", u=2)
+        x_ps = psum_keep.tile([P, 2, P], F32)
+        for u in range(2):
+            nc.tensor.transpose(x_ps[:, u, :], x_words[:, u, :], ident[:])
+        nc.scalar.copy(
+            out=x_grouped[:]
+            .bitcast(F32)
+            .rearrange("p (k b u) -> p k b u", k=PASSES, u=2)[:, :, 0:B, :],
+            in_=x_ps[:].rearrange("p u (b k) -> p k b u", k=PASSES),
+        )
         x_codes = keep.tile([P, PASSES, P], U32, align_bytes=64)
         x_scales = keep.tile([P, PASSES, P], U8, align_bytes=64)
 
         def quantise_x():
             nc.vector.quantize_mx(
-                out=x_codes[:].rearrange("p g b -> p (g b)").bitcast(FP8X4),
-                scales=x_scales[:].rearrange("p g b -> p (g b)"),
+                out=x_codes[:].rearrange("p k b -> p (k b)").bitcast(FP8X4),
+                scales=x_scales[:].rearrange("p k b -> p (k b)"),
                 in_=x_grouped[:],
             )
 
         acc = psum_keep.tile([P, PLACES, O], F32)
         w_grouped = {}
 
-        def transpose_place(h, w):
-            i0, j0 = 1 - w, 1 - h
-            for n in range(ROUNDS):
-                w_sorted = per_round.tile([P, TAPS * C_ROUND], BF16)
+        def bring_in(n):
+            for a in range(PAIR * n, PAIR * (n + 1)):
+                h, w = divmod(a // PASSES, E)
+                i0, j0 = 1 - w, 1 - h
+                w_sorted = per_pass.tile([P, TAPS * C_PASS], BF16)
                 nc.vector.tensor_copy(
-                    out=w_sorted[:].rearrange("o (g i j c) -> o g i c j", g=2, i=E, j=E),
-                    in_=w_raw[h, w, n][:].rearrange(
-                        "o (g c i j) -> o g i c j", g=2, i=KERNEL, j=KERNEL
-                    )[:, :, i0 : i0 + E, :, j0 : j0 + E],
+                    out=w_sorted[:].rearrange("o (i j c) -> o i c j", i=E, j=E),
+                    in_=w_raw[a].rearrange("o (c i j) -> o i c j", i=KERNEL, j=KERNEL)[
+                        :, i0 : i0 + E, :, j0 : j0 + E
+                    ],
                 )
-                w_words = w_sorted[:].bitcast(F32).rearrange("o (g r m) -> o g r m", g=2, r=E)
-                w_ps = psum_t.tile([P, E, 2, O], F32)
-                for r in range(E):
-                    for g in range(2):
-                        nc.tensor.transpose(w_ps[:, r, g, :], w_words[:, g, r, :], ident[:])
-                w_grouped[h, w, n] = per_round.tile(
-                    [P, E * O * PACK], BF16, align_bytes=64, name="w_grouped"
-                )
+                w_words = w_sorted[:].bitcast(F32).rearrange("o (m u) -> o u m", u=2)
+                w_ps = psum_t.tile([P, 2, O], F32)
+                for u in range(2):
+                    nc.tensor.transpose(w_ps[:, u, :], w_words[:, u, :], ident[:])
+                w_grouped[a] = per_pass.tile([P, O * PACK], BF16, align_bytes=64, name="w_grouped")
                 nc.scalar.copy(
-                    out=w_grouped[h, w, n][:]
-                    .bitcast(F32)
-                    .rearrange("p (r o g) -> p r o g", r=E, g=2),
-                    in_=w_ps[:].rearrange("p r g o -> p r o g"),
+                    out=w_grouped[a][:].bitcast(F32).rearrange("p (o u) -> p o u", u=2),
+                    in_=w_ps[:].rearrange("p u o -> p o u"),
                 )
 
-        def multiply_place(h, w):
-            w_codes = {}
-            w_scales = {}
-            for n in range(ROUNDS):
-                w_codes[n] = per_round.tile([P, E, O], U32, align_bytes=64, name="w_codes")
-                w_scales[n] = per_round.tile([P, E, O], U8, align_bytes=64, name="w_scales")
+        def multiply(n):
+            for a in range(PAIR * n, PAIR * (n + 1)):
+                s, k = divmod(a, PASSES)
+                w_codes = per_pass.tile([P, O], U32, align_bytes=64)
+                w_scales = per_pass.tile([P, O], U8, align_bytes=64)
                 nc.vector.quantize_mx(
-                    out=w_codes[n][:].rearrange("p r o -> p (r o)").bitcast(FP8X4),
-                    scales=w_scales[n][:].rearrange("p r o -> p (r o)"),
-                    in_=w_grouped[h, w, n][:],
+                    out=w_codes[:].bitcast(FP8X4), scales=w_scales[:], in_=w_grouped[a][:]
                 )
-            for k in range(PASSES):
-                n, r = divmod(k, E)
                 nc.tensor.matmul_mx(
-                    out=acc[:, h * E + w, :],
+                    out=acc[:, s, :],
                     lhsT=x_codes[:, k, :].bitcast(FP8X4),
                     lhsT_scale=x_scales[:, k, :],
-                    rhs=w_codes[n][:, r, :].bitcast(FP8X4),
-                    rhs_scale=w_scales[n][:, r, :],
+                    rhs=w_codes[:].bitcast(FP8X4),
+                    rhs_scale=w_scales[:],
                     start=(k == 0),
                     stop=(k == PASSES - 1),
                 )
 
-        places = [(h, w) for h in range(E) for w in range(E)]
-        transpose_place(*places[0])
+        for n in range(LAG):
+            bring_in(n)
         quantise_x()
-        for s in range(1, PLACES):
-            transpose_place(*places[s])
-            multiply_place(*places[s - 1])
-        multiply_place(*places[PLACES - 1])
+        for n in range(LAG, ROUNDS):
+            multiply(n - LAG)
+            bring_in(n)
+        for n in range(ROUNDS - LAG, ROUNDS):
+            multiply(n)
 
         result = keep.tile([B, O, PLACES], F32)
         nc.scalar.copy(out=result[:], in_=acc[0:B, :, :].rearrange("b s o -> b o s"))

@@ -109,20 +109,26 @@ def tile_locallyconnected2d_s_kernel(tc, x, weights, out):
                     in_=w_ps[:].rearrange("p u o -> p o u"),
                 )
 
+        w_codes = {}
+        w_scales = {}
+
+        def quantise(n):
+            for a in range(PAIR * n, PAIR * (n + 1)):
+                w_codes[a] = per_pass.tile([P, O], U32, align_bytes=64, name="w_codes")
+                w_scales[a] = per_pass.tile([P, O], U8, align_bytes=64, name="w_scales")
+                nc.vector.quantize_mx(
+                    out=w_codes[a][:].bitcast(FP8X4), scales=w_scales[a][:], in_=w_grouped[a][:]
+                )
+
         def multiply(n):
             for a in range(PAIR * n, PAIR * (n + 1)):
                 s, k = divmod(a, PASSES)
-                w_codes = per_pass.tile([P, O], U32, align_bytes=64)
-                w_scales = per_pass.tile([P, O], U8, align_bytes=64)
-                nc.vector.quantize_mx(
-                    out=w_codes[:].bitcast(FP8X4), scales=w_scales[:], in_=w_grouped[a][:]
-                )
                 nc.tensor.matmul_mx(
                     out=acc[:, s, :],
                     lhsT=x_codes[:, k, :].bitcast(FP8X4),
                     lhsT_scale=x_scales[:, k, :],
-                    rhs=w_codes[:].bitcast(FP8X4),
-                    rhs_scale=w_scales[:],
+                    rhs=w_codes[a][:].bitcast(FP8X4),
+                    rhs_scale=w_scales[a][:],
                     start=(k == 0),
                     stop=(k == PASSES - 1),
                 )
@@ -131,9 +137,13 @@ def tile_locallyconnected2d_s_kernel(tc, x, weights, out):
             bring_in(n)
         quantise_x()
         for n in range(LAG, ROUNDS):
-            multiply(n - LAG)
+            quantise(n - LAG)
             bring_in(n)
+            if n % 2 == 1:
+                multiply(n - LAG - 1)
+                multiply(n - LAG)
         for n in range(ROUNDS - LAG, ROUNDS):
+            quantise(n)
             multiply(n)
 
         result = keep.tile([B, O, PLACES], F32)

@@ -15,12 +15,16 @@ P = 128
 PACK = 4
 TAPS = E * E
 PLACES = E * E
-C_PASS = P * PACK // TAPS
-PASSES = C // C_PASS
-RAW_COLS = C_PASS * KERNEL * KERNEL
+PASSES = 4
+N_PASSES = PLACES * PASSES
+CHUNK = 64
+CHUNKS = 4
+CHUNK_RAW = CHUNK * KERNEL * KERNEL
+CHUNK_SORTED = CHUNK * TAPS
 PAIR = 2
-ROUNDS = PLACES * PASSES // PAIR
+ROUNDS = N_PASSES // PAIR
 LAG = 2
+LAST_LOADS = ((0, 2), (2, 3), (3, 4))
 
 FLOPS = 2 * B * O * PLACES * TAPS * C
 BYTES = 2 * (PLACES * TAPS * O * C) + 2 * (B * C * TAPS) + 4 * (B * O * PLACES)
@@ -30,51 +34,57 @@ def tile_locallyconnected2d_s_kernel(tc, x, weights, out):
     nc = tc.nc
     with ExitStack() as ctx:
         keep = ctx.enter_context(tc.tile_pool(name="keep", bufs=1))
-        per_pass = ctx.enter_context(tc.tile_pool(name="per_pass", bufs=PLACES * PASSES))
+        per_load = ctx.enter_context(
+            tc.tile_pool(name="per_load", bufs=ROUNDS - 1 + len(LAST_LOADS))
+        )
+        per_pass = ctx.enter_context(tc.tile_pool(name="per_pass", bufs=N_PASSES))
         psum_t = ctx.enter_context(tc.psum_pool(name="psum_t", bufs=6))
         psum_keep = ctx.enter_context(tc.psum_pool(name="psum_keep", bufs=1))
 
-        x_raw = keep.tile([P, C_PASS * TAPS], BF16)
+        x_raw = keep.tile([P, PAIR * CHUNK_SORTED], BF16)
         nc.sync.dma_start(
-            out=x_raw[:], in_=x.rearrange("b (k c) r q -> (b k) (c r q)", k=PASSES)
+            out=x_raw[:], in_=x.rearrange("b (f c) r q -> (b f) (c r q)", f=PASSES)
         )
         w_rows = weights.rearrange("h w o c i j -> (h w) o (c i j)")
         w_raw = {}
         for n in range(ROUNDS):
-            passes_a_load = 1 if n == ROUNDS - 1 else PAIR
-            for first in range(PAIR * n, PAIR * (n + 1), passes_a_load):
-                s, k = divmod(first, PASSES)
-                w_load = per_pass.tile([P, passes_a_load * RAW_COLS], BF16)
+            w_raw[n] = []
+            s, a = divmod(n, 2)
+            for q0, q1 in LAST_LOADS if n == ROUNDS - 1 else ((0, CHUNKS),):
+                w_load = per_load.tile([P, (q1 - q0) * CHUNK_RAW], BF16)
                 nc.sync.dma_start(
                     out=w_load[:],
-                    in_=w_rows[s, :, k * RAW_COLS : (k + passes_a_load) * RAW_COLS],
+                    in_=w_rows[s, :, (CHUNKS * a + q0) * CHUNK_RAW : (CHUNKS * a + q1) * CHUNK_RAW],
                 )
-                for g in range(passes_a_load):
-                    w_raw[first + g] = w_load[:, g * RAW_COLS : (g + 1) * RAW_COLS]
+                w_raw[n].append((q0, q1, w_load))
 
         ident = keep.tile([P, P], F32)
         make_identity(nc, ident[:])
 
         ctx.enter_context(tc.manual_schedule())
 
-        x_grouped = keep.tile([P, PASSES * P * PACK], BF16, align_bytes=64)
+        x_grouped = keep.tile([P, PASSES, P * PACK], BF16, align_bytes=64)
         nc.vector.memset(x_grouped[:].bitcast(I32), 0)
 
-        x_sorted = keep.tile([P, TAPS * C_PASS], BF16)
+        x_sorted = keep.tile([P, PAIR * CHUNK_SORTED], BF16)
         nc.vector.tensor_copy(
-            out=x_sorted[:].rearrange("p (t c) -> p t c", t=TAPS),
-            in_=x_raw[:].rearrange("p (c t) -> p t c", t=TAPS),
+            out=x_sorted[:].rearrange("p (g t c) -> p g t c", g=PAIR, t=TAPS),
+            in_=x_raw[:].rearrange("p (g c t) -> p g t c", g=PAIR, t=TAPS),
         )
-        x_words = x_sorted[:].bitcast(F32).rearrange("p (m u) -> p u m", u=2)
-        x_ps = psum_keep.tile([P, 2, P], F32)
-        for u in range(2):
-            nc.tensor.transpose(x_ps[:, u, :], x_words[:, u, :], ident[:])
-        nc.scalar.copy(
-            out=x_grouped[:]
-            .bitcast(F32)
-            .rearrange("p (k b u) -> p k b u", k=PASSES, u=2)[:, :, 0:B, :],
-            in_=x_ps[:].rearrange("p u (b k) -> p k b u", k=PASSES),
-        )
+        x_ps = psum_keep.tile([P, PAIR, P], F32)
+        for g in range(PAIR):
+            nc.tensor.transpose(
+                x_ps[:, g, :],
+                x_sorted[:, g * CHUNK_SORTED : (g + 1) * CHUNK_SORTED].bitcast(F32),
+                ident[:],
+            )
+        for a in range(2):
+            nc.scalar.copy(
+                out=x_grouped[:]
+                .bitcast(F32)[:, PAIR * a : PAIR * (a + 1), 0 : 2 * B]
+                .rearrange("p g (b u) -> p g b u", u=2),
+                in_=x_ps[:].rearrange("p g (b a u) -> p a g b u", a=2, u=2)[:, a],
+            )
         x_codes = keep.tile([P, PASSES, P], U32, align_bytes=64)
         x_scales = keep.tile([P, PASSES, P], U8, align_bytes=64)
 
@@ -82,35 +92,65 @@ def tile_locallyconnected2d_s_kernel(tc, x, weights, out):
             nc.vector.quantize_mx(
                 out=x_codes[:].rearrange("p k b -> p (k b)").bitcast(FP8X4),
                 scales=x_scales[:].rearrange("p k b -> p (k b)"),
-                in_=x_grouped[:],
+                in_=x_grouped[:].rearrange("p k c -> p (k c)"),
             )
 
         acc = psum_keep.tile([P, PLACES, O], F32)
+        w_sorted = {}
+        w_ps = {}
         w_grouped = {}
-
-        def bring_in(n):
-            for a in range(PAIR * n, PAIR * (n + 1)):
-                h, w = divmod(a // PASSES, E)
-                i0, j0 = 1 - w, 1 - h
-                w_sorted = per_pass.tile([P, TAPS * C_PASS], BF16)
-                nc.vector.tensor_copy(
-                    out=w_sorted[:].rearrange("o (i j c) -> o i c j", i=E, j=E),
-                    in_=w_raw[a].rearrange("o (c i j) -> o i c j", i=KERNEL, j=KERNEL)[
-                        :, i0 : i0 + E, :, j0 : j0 + E
-                    ],
-                )
-                w_words = w_sorted[:].bitcast(F32).rearrange("o (m u) -> o u m", u=2)
-                w_ps = psum_t.tile([P, 2, O], F32)
-                for u in range(2):
-                    nc.tensor.transpose(w_ps[:, u, :], w_words[:, u, :], ident[:])
-                w_grouped[a] = per_pass.tile([P, O * PACK], BF16, align_bytes=64, name="w_grouped")
-                nc.scalar.copy(
-                    out=w_grouped[a][:].bitcast(F32).rearrange("p (o u) -> p o u", u=2),
-                    in_=w_ps[:].rearrange("p u o -> p o u"),
-                )
-
         w_codes = {}
         w_scales = {}
+
+        def sort_taps(n, load):
+            h, w = divmod(n // 2, E)
+            i0, j0 = 1 - w, 1 - h
+            q0, q1, w_load = w_raw[n][load]
+            dst = w_sorted[n][:, q0:q1, :].rearrange("o q (i j c) -> o i q c j", i=E, j=E)
+            src = w_load[:].rearrange("o (q c i j) -> o i q c j", c=CHUNK, i=KERNEL, j=KERNEL)
+            if q1 - q0 == 1:
+                nc.vector.tensor_copy(
+                    out=dst[:, :, 0, :, :], in_=src[:, i0 : i0 + E, 0, :, j0 : j0 + E]
+                )
+            else:
+                for i in range(E):
+                    nc.vector.tensor_copy(out=dst[:, i], in_=src[:, i0 + i, :, :, j0 : j0 + E])
+
+        def transpose(n, q):
+            u, g = divmod(q, PAIR)
+            nc.tensor.transpose(
+                w_ps[PAIR * n + g][:, u, :], w_sorted[n][:, q, :].bitcast(F32), ident[:]
+            )
+
+        def lay_out(a):
+            nc.scalar.copy(
+                out=w_grouped[a][:].bitcast(F32).rearrange("p (o u) -> p o u", u=2),
+                in_=w_ps[a][:].rearrange("p u o -> p o u"),
+            )
+
+        def open_round(n):
+            w_sorted[n] = per_load.tile([P, CHUNKS, CHUNK_SORTED], BF16, name="w_sorted")
+            for a in range(PAIR * n, PAIR * (n + 1)):
+                w_ps[a] = psum_t.tile([P, 2, O], F32, name="w_ps")
+                w_grouped[a] = per_pass.tile([P, O * PACK], BF16, align_bytes=64, name="w_grouped")
+
+        def bring_in(n):
+            open_round(n)
+            sort_taps(n, 0)
+            for g in range(PAIR):
+                transpose(n, g)
+                transpose(n, PAIR + g)
+                lay_out(PAIR * n + g)
+
+        def bring_in_last(n):
+            open_round(n)
+            sort_taps(n, 0)
+            transpose(n, 0)
+            transpose(n, 1)
+            for g in range(PAIR):
+                sort_taps(n, 1 + g)
+                transpose(n, PAIR + g)
+                lay_out(PAIR * n + g)
 
         def quantise(n):
             for a in range(PAIR * n, PAIR * (n + 1)):
@@ -138,7 +178,10 @@ def tile_locallyconnected2d_s_kernel(tc, x, weights, out):
         quantise_x()
         for n in range(LAG, ROUNDS):
             quantise(n - LAG)
-            bring_in(n)
+            if n == ROUNDS - 1:
+                bring_in_last(n)
+            else:
+                bring_in(n)
             if n % 2 == 1:
                 multiply(n - LAG - 1)
                 multiply(n - LAG)

@@ -56,7 +56,7 @@ def tile_locallyconnected2d_s_kernel(tc, x, weights, out):
                     out=w_load[:],
                     in_=w_rows[s, :, (CHUNKS * a + q0) * CHUNK_RAW : (CHUNKS * a + q1) * CHUNK_RAW],
                 )
-                w_raw[n].append((q0, q1, w_load))
+                w_raw[n].append((q0, w_load))
 
         ident = keep.tile([P, P], F32)
         make_identity(nc, ident[:])
@@ -102,24 +102,27 @@ def tile_locallyconnected2d_s_kernel(tc, x, weights, out):
         w_codes = {}
         w_scales = {}
 
-        def sort_taps(n, load):
+        def sort_taps(n, load, g, halves):
             h, w = divmod(n // 2, E)
             i0, j0 = 1 - w, 1 - h
-            q0, q1, w_load = w_raw[n][load]
-            dst = w_sorted[n][:, q0:q1, :].rearrange("o q (i j c) -> o i q c j", i=E, j=E)
+            q0, w_load = w_raw[n][load]
+            dst = w_sorted[PAIR * n + g][:].rearrange("o u (i j c) -> o i u c j", i=E, j=E)
             src = w_load[:].rearrange("o (q c i j) -> o i q c j", c=CHUNK, i=KERNEL, j=KERNEL)
-            if q1 - q0 == 1:
+            if len(halves) == 1:
+                u = halves[0]
                 nc.vector.tensor_copy(
-                    out=dst[:, :, 0, :, :], in_=src[:, i0 : i0 + E, 0, :, j0 : j0 + E]
+                    out=dst[:, :, u, :, :],
+                    in_=src[:, i0 : i0 + E, PAIR * u + g - q0, :, j0 : j0 + E],
                 )
             else:
-                for i in range(E):
-                    nc.vector.tensor_copy(out=dst[:, i], in_=src[:, i0 + i, :, :, j0 : j0 + E])
+                nc.vector.tensor_copy(
+                    out=dst, in_=src[:, i0 : i0 + E, g:CHUNKS:PAIR, :, j0 : j0 + E]
+                )
 
         def transpose(n, q):
             u, g = divmod(q, PAIR)
             nc.tensor.transpose(
-                w_ps[PAIR * n + g][:, u, :], w_sorted[n][:, q, :].bitcast(F32), ident[:]
+                w_ps[PAIR * n + g][:, u, :], w_sorted[PAIR * n + g][:, u, :].bitcast(F32), ident[:]
             )
 
         def lay_out(a):
@@ -129,26 +132,26 @@ def tile_locallyconnected2d_s_kernel(tc, x, weights, out):
             )
 
         def open_round(n):
-            w_sorted[n] = per_load.tile([P, CHUNKS, CHUNK_SORTED], BF16, name="w_sorted")
             for a in range(PAIR * n, PAIR * (n + 1)):
+                w_sorted[a] = per_pass.tile([P, 2, CHUNK_SORTED], BF16, name="w_sorted")
                 w_ps[a] = psum_t.tile([P, 2, O], F32, name="w_ps")
                 w_grouped[a] = per_pass.tile([P, O * PACK], BF16, align_bytes=64, name="w_grouped")
 
         def bring_in(n):
             open_round(n)
-            sort_taps(n, 0)
             for g in range(PAIR):
+                sort_taps(n, 0, g, (0, 1))
                 transpose(n, g)
                 transpose(n, PAIR + g)
                 lay_out(PAIR * n + g)
 
         def bring_in_last(n):
             open_round(n)
-            sort_taps(n, 0)
-            transpose(n, 0)
-            transpose(n, 1)
             for g in range(PAIR):
-                sort_taps(n, 1 + g)
+                sort_taps(n, 0, g, (0,))
+                transpose(n, g)
+            for g in range(PAIR):
+                sort_taps(n, 1 + g, g, (1,))
                 transpose(n, PAIR + g)
                 lay_out(PAIR * n + g)
 
@@ -176,17 +179,16 @@ def tile_locallyconnected2d_s_kernel(tc, x, weights, out):
         for n in range(LAG):
             bring_in(n)
         quantise_x()
-        for n in range(LAG, ROUNDS):
+        for n in range(LAG, ROUNDS - 1):
             quantise(n - LAG)
-            if n == ROUNDS - 1:
-                bring_in_last(n)
-            else:
-                bring_in(n)
             if n % 2 == 1:
                 multiply(n - LAG - 1)
                 multiply(n - LAG)
-        for n in range(ROUNDS - LAG, ROUNDS):
+            bring_in(n)
+        bring_in_last(ROUNDS - 1)
+        for n in range(ROUNDS - 1 - LAG, ROUNDS):
             quantise(n)
+        for n in range(ROUNDS - 2 - LAG, ROUNDS):
             multiply(n)
 
         result = keep.tile([B, O, PLACES], F32)

from contextlib import ExitStack

import concourse.mybir as mybir
from concourse.masks import make_identity

F32 = mybir.dt.float32
BF16 = mybir.dt.bfloat16
I32 = mybir.dt.int32
U32 = mybir.dt.uint32
U8 = mybir.dt.uint8
FP8X4 = mybir.dt.float8_e4m3fn_x4

B, C, O, E, KERNEL = 32, 512, 128, 2, 3
P = 128
PACK = 4
TAPS = E * E
PLACES = E * E
PASSES = 4
N_PASSES = PLACES * PASSES
CHUNK = 64
CHUNKS = 4
CHUNK_RAW = CHUNK * KERNEL * KERNEL
CHUNK_SORTED = CHUNK * TAPS
PAIR = 2
ROUNDS = N_PASSES // PAIR
LAG = 2
LAST_LOADS = ((0, 2), (2, 3), (3, 4))

FLOPS = 2 * B * O * PLACES * TAPS * C
BYTES = 2 * (PLACES * TAPS * O * C) + 2 * (B * C * TAPS) + 4 * (B * O * PLACES)


def tile_locallyconnected2d_s_kernel(tc, x, weights, out):
    nc = tc.nc
    with ExitStack() as ctx:
        keep = ctx.enter_context(tc.tile_pool(name="keep", bufs=1))
        per_load = ctx.enter_context(
            tc.tile_pool(name="per_load", bufs=ROUNDS - 1 + len(LAST_LOADS))
        )
        per_pass = ctx.enter_context(tc.tile_pool(name="per_pass", bufs=N_PASSES))
        psum_t = ctx.enter_context(tc.psum_pool(name="psum_t", bufs=6))
        psum_keep = ctx.enter_context(tc.psum_pool(name="psum_keep", bufs=1))

        x_raw = keep.tile([P, PAIR * CHUNK_SORTED], BF16)
        nc.sync.dma_start(
            out=x_raw[:], in_=x.rearrange("b (f c) r q -> (b f) (c r q)", f=PASSES)
        )
        w_rows = weights.rearrange("h w o c i j -> (h w) o (c i j)")
        w_raw = {}
        for n in range(ROUNDS):
            w_raw[n] = []
            s, a = divmod(n, 2)
            for q0, q1 in LAST_LOADS if n == ROUNDS - 1 else ((0, CHUNKS),):
                w_load = per_load.tile([P, (q1 - q0) * CHUNK_RAW], BF16)
                nc.sync.dma_start(
                    out=w_load[:],
                    in_=w_rows[s, :, (CHUNKS * a + q0) * CHUNK_RAW : (CHUNKS * a + q1) * CHUNK_RAW],
                )
                w_raw[n].append((q0, w_load))

        ident = keep.tile([P, P], F32)
        make_identity(nc, ident[:])

        ctx.enter_context(tc.manual_schedule())

        x_grouped = keep.tile([P, PASSES, P * PACK], BF16, align_bytes=64)
        nc.vector.memset(x_grouped[:].bitcast(I32), 0)

        x_sorted = keep.tile([P, PAIR * CHUNK_SORTED], BF16)
        nc.vector.tensor_copy(
            out=x_sorted[:].rearrange("p (g t c) -> p g t c", g=PAIR, t=TAPS),
            in_=x_raw[:].rearrange("p (g c t) -> p g t c", g=PAIR, t=TAPS),
        )
        x_ps = psum_keep.tile([P, PAIR, P], F32)
        for g in range(PAIR):
            nc.tensor.transpose(
                x_ps[:, g, :],
                x_sorted[:, g * CHUNK_SORTED : (g + 1) * CHUNK_SORTED].bitcast(F32),
                ident[:],
            )
        for a in range(2):
            nc.scalar.copy(
                out=x_grouped[:]
                .bitcast(F32)[:, PAIR * a : PAIR * (a + 1), 0 : 2 * B]
                .rearrange("p g (b u) -> p g b u", u=2),
                in_=x_ps[:].rearrange("p g (b a u) -> p a g b u", a=2, u=2)[:, a],
            )
        x_codes = keep.tile([P, PASSES, P], U32, align_bytes=64)
        x_scales = keep.tile([P, PASSES, P], U8, align_bytes=64)

        def quantise_x():
            nc.vector.quantize_mx(
                out=x_codes[:].rearrange("p k b -> p (k b)").bitcast(FP8X4),
                scales=x_scales[:].rearrange("p k b -> p (k b)"),
                in_=x_grouped[:].rearrange("p k c -> p (k c)"),
            )

        acc = psum_keep.tile([P, PLACES, O], F32)
        w_sorted = {}
        w_ps = {}
        w_grouped = {}
        w_codes = {}
        w_scales = {}

        def sort_taps(n, load, g, halves):
            h, w = divmod(n // 2, E)
            i0, j0 = 1 - w, 1 - h
            q0, w_load = w_raw[n][load]
            dst = w_sorted[PAIR * n + g][:].rearrange("o u (i j c) -> o i u c j", i=E, j=E)
            src = w_load[:].rearrange("o (q c i j) -> o i q c j", c=CHUNK, i=KERNEL, j=KERNEL)
            if len(halves) == 1:
                u = halves[0]
                nc.vector.tensor_copy(
                    out=dst[:, :, u, :, :],
                    in_=src[:, i0 : i0 + E, PAIR * u + g - q0, :, j0 : j0 + E],
                )
            else:
                nc.vector.tensor_copy(
                    out=dst, in_=src[:, i0 : i0 + E, g:CHUNKS:PAIR, :, j0 : j0 + E]
                )

        def transpose(n, q):
            u, g = divmod(q, PAIR)
            nc.tensor.transpose(
                w_ps[PAIR * n + g][:, u, :], w_sorted[PAIR * n + g][:, u, :].bitcast(F32), ident[:]
            )

        def lay_out(a):
            nc.scalar.copy(
                out=w_grouped[a][:].bitcast(F32).rearrange("p (o u) -> p o u", u=2),
                in_=w_ps[a][:].rearrange("p u o -> p o u"),
            )

        def open_round(n):
            for a in range(PAIR * n, PAIR * (n + 1)):
                w_sorted[a] = per_pass.tile([P, 2, CHUNK_SORTED], BF16, name="w_sorted")
                w_ps[a] = psum_t.tile([P, 2, O], F32, name="w_ps")
                w_grouped[a] = per_pass.tile([P, O * PACK], BF16, align_bytes=64, name="w_grouped")

        def bring_in(n):
            open_round(n)
            for g in range(PAIR):
                sort_taps(n, 0, g, (0, 1))
                transpose(n, g)
                transpose(n, PAIR + g)
                lay_out(PAIR * n + g)

        def bring_in_last(n):
            open_round(n)
            for g in range(PAIR):
                sort_taps(n, 0, g, (0,))
                transpose(n, g)
            for g in range(PAIR):
                sort_taps(n, 1 + g, g, (1,))
                transpose(n, PAIR + g)
                lay_out(PAIR * n + g)

        def quantise(n):
            for a in range(PAIR * n, PAIR * (n + 1)):
                w_codes[a] = per_pass.tile([P, O], U32, align_bytes=64, name="w_codes")
                w_scales[a] = per_pass.tile([P, O], U8, align_bytes=64, name="w_scales")
                nc.vector.quantize_mx(
                    out=w_codes[a][:].bitcast(FP8X4), scales=w_scales[a][:], in_=w_grouped[a][:]
                )

        def multiply(n):
            for a in range(PAIR * n, PAIR * (n + 1)):
                s, k = divmod(a, PASSES)
                nc.tensor.matmul_mx(
                    out=acc[:, s, :],
                    lhsT=x_codes[:, k, :].bitcast(FP8X4),
                    lhsT_scale=x_scales[:, k, :],
                    rhs=w_codes[a][:].bitcast(FP8X4),
                    rhs_scale=w_scales[a][:],
                    start=(k == 0),
                    stop=(k == PASSES - 1),
                )

        for n in range(LAG):
            bring_in(n)
        quantise_x()
        for n in range(LAG, ROUNDS - 1):
            quantise(n - LAG)
            if n % 2 == 1:
                multiply(n - LAG - 1)
                multiply(n - LAG)
            bring_in(n)
        bring_in_last(ROUNDS - 1)
        for n in range(ROUNDS - 1 - LAG, ROUNDS):
            quantise(n)
        for n in range(ROUNDS - 2 - LAG, ROUNDS):
            multiply(n)

        result = keep.tile([B, O, PLACES], F32)
        nc.scalar.copy(out=result[:], in_=acc[0:B, :, :].rearrange("b s o -> b o s"))
        nc.sync.dma_start(
            out=out.rearrange("b o h w -> b (o h w)"),
            in_=result[:].rearrange("b o s -> b (o s)"),
        )
